import numpy as np
import ml_dtypes


def mxq(x, axis, fmt="e4m3"):
    dtype, down = {"e4m3": (ml_dtypes.float8_e4m3fn, 7), "e5m2": (ml_dtypes.float8_e5m2, 14)}[fmt]
    v = np.moveaxis(np.asarray(x, np.float32).astype(ml_dtypes.bfloat16).astype(np.float64), axis, -1)
    blocks = v.reshape(v.shape[:-1] + (-1, 32))
    amax = np.abs(blocks).max(-1, keepdims=True)
    byte = np.maximum(np.where(amax > 0, np.frexp(amax)[1] - 1 + 127, 0) - down, 1)
    scale = np.exp2(byte - 127.0)
    codes = (blocks / scale).astype(np.float32).astype(dtype).astype(np.float64)
    return np.moveaxis((codes * scale).reshape(v.shape), -1, axis)


WIDE = False


def mx_kscale(k):
    if not WIDE:
        return np.ones(k)
    levels = np.array([10, -10, 5, -5, 0])
    a = np.random.permutation(np.resize(levels, k // 512 * 4)).reshape(k // 512, 4)
    idx = np.arange(k)
    return np.exp2(a[idx // 512, idx % 128 // 32])


BF16 = ml_dtypes.bfloat16


def bf(x):
    return np.asarray(x, np.float32).astype(BF16)


def f64(x):
    return np.asarray(x).astype(np.float64)


B, N, D, H, DH = 2, 512, 1024, 16, 64
INNER = H * DH


def dpfp(u):
    u2 = np.concatenate([np.maximum(u, 0.0), np.maximum(-u, 0.0)], axis=-1)
    return u2 * np.roll(u2, 1, axis=-1)


def heads(t):
    return t.reshape(B, N, H, DH).transpose(0, 2, 1, 3)


def setup_inputs():
    s = mx_kscale(D)
    return {"x": bf(np.random.standard_normal((B, N, D)) * s),
            "w_qk": bf(np.random.standard_normal((D, 2 * INNER)) / np.sqrt(D) / s[:, None])}


def reference(x, w_qk):
    qk = mxq(f64(x), 2, "e4m3") @ mxq(f64(w_qk), 0, "e4m3")
    q, k = np.split(qk, 2, axis=-1)
    q, k = dpfp(heads(q)), dpfp(heads(k))
    return q / q.sum(-1, keepdims=True), k / k.sum(-1, keepdims=True)

@@ -1,0 +1,222 @@
+from contextlib import ExitStack
+
+import concourse.masks as masks
+import concourse.mybir as mybir
+
+FLOPS = 2 * 1024 * 1024 * 2048
+
+F32 = mybir.dt.float32
+BF16 = mybir.dt.bfloat16
+U32 = mybir.dt.uint32
+U8 = mybir.dt.uint8
+FP8X4 = mybir.dt.float8_e4m3fn_x4
+ALU = mybir.AluOpType
+ACT = mybir.ActivationFunctionType
+
+P = 128
+PINNED = True
+N_BANKS = 32
+
+
+def tile_dpfpattention_pa_kernel(tc, x, w_qk, out_0, out_1):
+    nc = tc.nc
+    outs = (out_0, out_1)
+    with ExitStack() as ctx:
+        keep = ctx.enter_context(tc.tile_pool(name="keep", bufs=1))
+        gx_pool = ctx.enter_context(tc.tile_pool(name="gx_pool", bufs=4))
+        gw_pool = ctx.enter_context(tc.tile_pool(name="gw_pool", bufs=2))
+        c_pool = ctx.enter_context(tc.tile_pool(name="c_pool", bufs=4))
+        pm_pool = ctx.enter_context(tc.tile_pool(name="pm_pool", bufs=6))
+        stat_pool = ctx.enter_context(tc.tile_pool(name="stat_pool", bufs=6))
+        o_pool = ctx.enter_context(tc.tile_pool(name="o_pool", bufs=3))
+        psum = ctx.enter_context(tc.psum_pool(name="psum", bufs=8))
+        if PINNED:
+            ctx.enter_context(tc.manual_schedule())
+
+        ident = keep.tile([P, P], F32, name="ident")
+        warm = keep.tile([P, 8], F32, name="warm")
+        x_sb = [keep.tile([P, 4, 1024], BF16, name="x_sb%d" % b) for b in range(2)]
+        w_sb = [keep.tile([P, 2, 4, 512], BF16, name="w_sb%d" % n) for n in range(4)]
+        xq = [[keep.tile([P, 256], U32, name="xq%d%d" % (b, t), align_bytes=64) for t in range(4)] for b in range(2)]
+        xs = [[keep.tile([P, 256], U8, name="xs%d%d" % (b, t), align_bytes=64) for t in range(4)] for b in range(2)]
+        wq = [[keep.tile([P, 512], U32, name="wq%d%d" % (n, g), align_bytes=64) for g in range(2)] for n in range(4)]
+        ws = [[keep.tile([P, 512], U8, name="ws%d%d" % (n, g), align_bytes=64) for g in range(2)] for n in range(4)]
+
+        live = {}
+
+        def load_x(b, t0, t1):
+            nc.sync.dma_start(
+                out=x_sb[b][:, t0:t1, :],
+                in_=x[b].rearrange("(p t) k -> p t k", t=4)[:, t0:t1, :],
+            )
+
+        def load_w(n, g):
+            nc.sync.dma_start(
+                out=w_sb[n][:, g],
+                in_=w_qk[512 * g : 512 * (g + 1), 512 * n : 512 * (n + 1)].rearrange("(p j) c -> p j c", j=4),
+            )
+
+        def transpose_x(b, t):
+            xt = psum.tile([P, 2, 2, P], F32, name="xt", tag="bank")
+            words = x_sb[b][:, t, :].bitcast(F32)
+            for g in range(2):
+                for u in range(2):
+                    nc.tensor.transpose(xt[:, g, u, :], words[:, 256 * g + u : 256 * (g + 1) : 2], ident[:])
+            live["xt", b, t] = xt
+
+        def evacuate_x(b, t):
+            gx = gx_pool.tile([P, 2, P, 4], BF16, name="gx", align_bytes=64)
+            nc.scalar.copy(out=gx[:].bitcast(F32), in_=live["xt", b, t][:].rearrange("p g u r -> p g r u"))
+            live["gx", b, t] = gx
+
+        def quantise_x(b, t):
+            nc.vector.quantize_mx(
+                out=xq[b][t][:].bitcast(FP8X4),
+                scales=xs[b][t][:],
+                in_=live["gx", b, t][:].rearrange("p g r j -> p (g r j)"),
+            )
+
+        def regroup_w(n, g):
+            if g == 0:
+                live["gw", n] = gw_pool.tile([P, 2, 512, 4], BF16, name="gw", align_bytes=64)
+            nc.vector.tensor_copy(
+                out=live["gw", n][:, g].rearrange("p (c i) j -> p c j i", i=4),
+                in_=w_sb[n][:, g].rearrange("p j (c i) -> p c j i", i=4),
+            )
+
+        def quantise_w(n, g):
+            nc.vector.quantize_mx(
+                out=wq[n][g][:].bitcast(FP8X4),
+                scales=ws[n][g][:],
+                in_=live["gw", n][:, g].rearrange("p c j -> p (c j)"),
+            )
+
+        def where(k):
+            unit, t = divmod(k, 4)
+            n, b = divmod(unit, 2)
+            return unit, n, b, t
+
+        def multiply(k):
+            unit, n, b, t = where(k)
+            u = psum.tile([P, 8, 64], F32, name="u", tag="bank")
+            for g in range(2):
+                nc.tensor.matmul_mx(
+                    out=u[:].rearrange("p h d -> p (h d)"),
+                    lhsT=xq[b][t][:, P * g : P * (g + 1)].bitcast(FP8X4),
+                    lhsT_scale=xs[b][t][:, P * g : P * (g + 1)],
+                    rhs=wq[n][g][:].bitcast(FP8X4),
+                    rhs_scale=ws[n][g][:],
+                    start=(g == 0),
+                    stop=(g == 1),
+                )
+            live["u", k] = u
+
+        def roll(k):
+            u = live["u", k]
+            c = c_pool.tile([P, 8, 64], F32, name="c")
+            nc.scalar.copy(out=c[:, :, 1:64], in_=u[:, :, 0:63])
+            nc.scalar.mul(out=c[:, :, 0:1], in_=u[:, :, 63:64], mul=-1.0)
+            live["c", k] = c
+
+        def product(k, half):
+            if half == 0:
+                live["pm", k] = pm_pool.tile([P, 8, P], F32, name="pm")
+            nc.vector.scalar_tensor_tensor(
+                out=live["pm", k][:, :, 64 * half : 64 * (half + 1)],
+                in0=live["u", k][:],
+                scalar=0.0,
+                in1=live["c", k][:],
+                op0=(ALU.max if half == 0 else ALU.min),
+                op1=ALU.mult,
+            )
+
+        def relu_sum(k):
+            pm = live["pm", k]
+            ssum = stat_pool.tile([P, 8], F32, name="ssum")
+            for h in range(8):
+                nc.scalar.activation(out=pm[:, h, :], in_=pm[:, h, :], func=ACT.Relu, accum_out=ssum[:, h : h + 1])
+            live["ssum", k] = ssum
+
+        def invert(k):
+            rinv = stat_pool.tile([P, 8], F32, name="rinv")
+            nc.vector.reciprocal(out=rinv[:], in_=live["ssum", k][:])
+            live["rinv", k] = rinv
+
+        def scale(k):
+            unit, n, b, t = where(k)
+            if t == 0:
+                live["o", unit] = o_pool.tile([P, 8, 4, P], F32, name="o")
+            o = live["o", unit]
+            for h in range(8):
+                nc.vector.tensor_scalar_mul(out=o[:, h, t, :], in0=live["pm", k][:, h, :], scalar1=live["rinv", k][:, h : h + 1])
+
+        def store(k):
+            unit, n, b, t = where(k)
+            heads = outs[n // 2][b, 8 * (n % 2) : 8 * (n % 2) + 8]
+            o = live["o", unit]
+            if unit == 7:
+                nc.sync.dma_start(out=heads.rearrange("h (p t) f -> t p h f", t=4)[t], in_=o[:, :, t, :])
+            elif t == 3:
+                nc.sync.dma_start(
+                    out=heads.rearrange("h (p t) f -> p h (t f)", t=4),
+                    in_=o[:].rearrange("p h t f -> p h (t f)"),
+                )
+
+        load_x(0, 0, 1)
+        load_w(0, 0)
+        load_w(0, 1)
+        load_x(0, 1, 4)
+        load_x(1, 0, 4)
+        for n in range(1, 4):
+            load_w(n, 0)
+            load_w(n, 1)
+
+        masks.make_identity(nc, ident[:])
+        nc.vector.memset(warm[:], 0.0)
+        nc.scalar.activation(out=warm[:], in_=warm[:], func=ACT.Relu)
+
+        transpose_x(0, 0)
+        evacuate_x(0, 0)
+        regroup_w(0, 0)
+        quantise_x(0, 0)
+        regroup_w(0, 1)
+        quantise_w(0, 0)
+        quantise_w(0, 1)
+        multiply(0)
+        roll(0)
+        product(0, 0)
+        product(0, 1)
+        for t in range(1, 4):
+            transpose_x(0, t)
+            evacuate_x(0, t)
+        for t in range(1, 4):
+            quantise_x(0, t)
+            multiply(t)
+        for t in range(4):
+            transpose_x(1, t)
+
+        for s in range(N_BANKS + 1):
+            if s + 1 < N_BANKS:
+                roll(s + 1)
+                product(s + 1, 0)
+            if 1 <= s <= 4:
+                evacuate_x(1, s - 1)
+            if s < N_BANKS:
+                relu_sum(s)
+            if s >= 1:
+                invert(s - 1)
+            if s + 1 < N_BANKS:
+                product(s + 1, 1)
+            if s >= 1:
+                scale(s - 1)
+                store(s - 1)
+            if 1 <= s <= 4:
+                quantise_x(1, s - 1)
+            n, piece = divmod(s + 7, 8)
+            if 1 <= n <= 3 and piece < 4:
+                if piece < 2:
+                    regroup_w(n, piece)
+                else:
+                    quantise_w(n, piece - 2)
+            if 4 <= s + 3 < N_BANKS:
+                multiply(s + 3)

@@ -26,7 +26,8 @@ def tile_dpfpattention_pa_kernel(tc, x, w_qk, out_0, out_1):
         gx_pool = ctx.enter_context(tc.tile_pool(name="gx_pool", bufs=4))
         gw_pool = ctx.enter_context(tc.tile_pool(name="gw_pool", bufs=2))
         c_pool = ctx.enter_context(tc.tile_pool(name="c_pool", bufs=4))
-        pm_pool = ctx.enter_context(tc.tile_pool(name="pm_pool", bufs=6))
+        v_pool = ctx.enter_context(tc.tile_pool(name="v_pool", bufs=6))
+        wn_pool = ctx.enter_context(tc.tile_pool(name="wn_pool", bufs=5))
         stat_pool = ctx.enter_context(tc.tile_pool(name="stat_pool", bufs=6))
         o_pool = ctx.enter_context(tc.tile_pool(name="o_pool", bufs=3))
         psum = ctx.enter_context(tc.psum_pool(name="psum", bufs=8))
@@ -91,6 +92,12 @@ def tile_dpfpattention_pa_kernel(tc, x, w_qk, out_0, out_1):
                 in_=live["gw", n][:, g].rearrange("p c j -> p (c j)"),
             )
 
+        def cross_on_gpsimd(k):
+            return k % 2 == 0
+
+        def normalise_on_scalar(k):
+            return k % 4 == 0
+
         def where(k):
             unit, t = divmod(k, 4)
             n, b = divmod(unit, 2)
@@ -113,28 +120,25 @@ def tile_dpfpattention_pa_kernel(tc, x, w_qk, out_0, out_1):
 
         def roll(k):
             u = live["u", k]
-            c = c_pool.tile([P, 8, 64], F32, name="c")
-            nc.scalar.copy(out=c[:, :, 1:64], in_=u[:, :, 0:63])
+            c = c_pool.tile([P, 8, 65], F32, name="c")
+            nc.scalar.copy(out=c[:, :, 1:65], in_=u[:])
             nc.scalar.mul(out=c[:, :, 0:1], in_=u[:, :, 63:64], mul=-1.0)
             live["c", k] = c
 
-        def product(k, half):
-            if half == 0:
-                live["pm", k] = pm_pool.tile([P, 8, P], F32, name="pm")
-            nc.vector.scalar_tensor_tensor(
-                out=live["pm", k][:, :, 64 * half : 64 * (half + 1)],
-                in0=live["u", k][:],
-                scalar=0.0,
-                in1=live["c", k][:],
-                op0=(ALU.max if half == 0 else ALU.min),
-                op1=ALU.mult,
-            )
+        def cross(k):
+            v = v_pool.tile([P, 8, 64], F32, name="v")
+            c = live["c", k]
+            if cross_on_gpsimd(k):
+                nc.gpsimd.tensor_tensor(out=v[:], in0=c[:, :, 1:65], in1=c[:, :, 0:64], op=ALU.mult)
+            else:
+                nc.vector.tensor_tensor(out=v[:], in0=live["u", k][:], in1=c[:, :, 0:64], op=ALU.mult)
+            live["v", k] = v
 
         def relu_sum(k):
-            pm = live["pm", k]
+            v = live["v", k]
             ssum = stat_pool.tile([P, 8], F32, name="ssum")
             for h in range(8):
-                nc.scalar.activation(out=pm[:, h, :], in_=pm[:, h, :], func=ACT.Relu, accum_out=ssum[:, h : h + 1])
+                nc.scalar.activation(out=v[:, h, :], in_=v[:, h, :], func=ACT.Relu, accum_out=ssum[:, h : h + 1])
             live["ssum", k] = ssum
 
         def invert(k):
@@ -142,13 +146,31 @@ def tile_dpfpattention_pa_kernel(tc, x, w_qk, out_0, out_1):
             nc.vector.reciprocal(out=rinv[:], in_=live["ssum", k][:])
             live["rinv", k] = rinv
 
-        def scale(k):
+        def normalise(k):
+            wn = wn_pool.tile([P, 8, 64], F32, name="wn")
+            v = live["v", k]
+            rinv = live["rinv", k]
+            if normalise_on_scalar(k):
+                for h in range(8):
+                    nc.scalar.activation(out=wn[:, h, :], in_=v[:, h, :], func=ACT.Copy, scale=rinv[:, h : h + 1])
+            else:
+                nc.gpsimd.tensor_tensor(
+                    out=wn[:], in0=v[:], in1=rinv[:].unsqueeze(2).to_broadcast([P, 8, 64]), op=ALU.mult
+                )
+            live["wn", k] = wn
+
+        def split(k, half):
             unit, n, b, t = where(k)
-            if t == 0:
+            if t == 0 and half == 0:
                 live["o", unit] = o_pool.tile([P, 8, 4, P], F32, name="o")
-            o = live["o", unit]
-            for h in range(8):
-                nc.vector.tensor_scalar_mul(out=o[:, h, t, :], in0=live["pm", k][:, h, :], scalar1=live["rinv", k][:, h : h + 1])
+            nc.vector.scalar_tensor_tensor(
+                out=live["o", unit][:, :, t, 64 * half : 64 * (half + 1)],
+                in0=live["u", k][:],
+                scalar=0.0,
+                in1=live["wn", k][:],
+                op0=(ALU.is_gt if half == 0 else ALU.is_lt),
+                op1=ALU.mult,
+            )
 
         def store(k):
             unit, n, b, t = where(k)
@@ -183,40 +205,48 @@ def tile_dpfpattention_pa_kernel(tc, x, w_qk, out_0, out_1):
         quantise_w(0, 0)
         quantise_w(0, 1)
         multiply(0)
-        roll(0)
-        product(0, 0)
-        product(0, 1)
         for t in range(1, 4):
             transpose_x(0, t)
-            evacuate_x(0, t)
-        for t in range(1, 4):
-            quantise_x(0, t)
-            multiply(t)
-        for t in range(4):
-            transpose_x(1, t)
 
-        for s in range(N_BANKS + 1):
-            if s + 1 < N_BANKS:
-                roll(s + 1)
-                product(s + 1, 0)
-            if 1 <= s <= 4:
-                evacuate_x(1, s - 1)
-            if s < N_BANKS:
-                relu_sum(s)
-            if s >= 1:
-                invert(s - 1)
-            if s + 1 < N_BANKS:
-                product(s + 1, 1)
-            if s >= 1:
-                scale(s - 1)
-                store(s - 1)
-            if 1 <= s <= 4:
-                quantise_x(1, s - 1)
-            n, piece = divmod(s + 7, 8)
+        def on(k):
+            return 0 <= k < N_BANKS
+
+        for s in range(N_BANKS + 5):
+            if on(s):
+                roll(s)
+            if s == 0:
+                for t in range(1, 4):
+                    evacuate_x(0, t)
+            if 2 <= s <= 5:
+                evacuate_x(1, s - 2)
+            if on(s) and cross_on_gpsimd(s):
+                cross(s)
+            if on(s - 1):
+                relu_sum(s - 1)
+            if on(s - 2):
+                invert(s - 2)
+                normalise(s - 2)
+            if on(s - 4):
+                split(s - 4, 0)
+            if on(s) and not cross_on_gpsimd(s):
+                cross(s)
+            if on(s - 4):
+                split(s - 4, 1)
+                store(s - 4)
+            if s == 0:
+                for t in range(1, 4):
+                    quantise_x(0, t)
+                multiply(1)
+            if 2 <= s <= 5:
+                quantise_x(1, s - 2)
+            n, piece = divmod(s + 6, 8)
             if 1 <= n <= 3 and piece < 4:
                 if piece < 2:
                     regroup_w(n, piece)
                 else:
                     quantise_w(n, piece - 2)
-            if 4 <= s + 3 < N_BANKS:
-                multiply(s + 3)
+            if on(s + 2):
+                multiply(s + 2)
+            if s == 1:
+                for t in range(4):
+                    transpose_x(1, t)

@@ -92,7 +92,7 @@ def tile_dpfpattention_pa_kernel(tc, x, w_qk, out_0, out_1):
                 in_=live["gw", n][:, g].rearrange("p c j -> p (c j)"),
             )
 
-        def cross_on_gpsimd(k):
+        def negative_on_gpsimd(k):
             return k % 2 == 0
 
         def normalise_on_scalar(k):
@@ -120,18 +120,15 @@ def tile_dpfpattention_pa_kernel(tc, x, w_qk, out_0, out_1):
 
         def roll(k):
             u = live["u", k]
-            c = c_pool.tile([P, 8, 65], F32, name="c")
-            nc.scalar.copy(out=c[:, :, 1:65], in_=u[:])
+            c = c_pool.tile([P, 8, 64], F32, name="c")
+            nc.scalar.copy(out=c[:, :, 1:64], in_=u[:, :, 0:63])
             nc.scalar.mul(out=c[:, :, 0:1], in_=u[:, :, 63:64], mul=-1.0)
             live["c", k] = c
 
         def cross(k):
             v = v_pool.tile([P, 8, 64], F32, name="v")
             c = live["c", k]
-            if cross_on_gpsimd(k):
-                nc.gpsimd.tensor_tensor(out=v[:], in0=c[:, :, 1:65], in1=c[:, :, 0:64], op=ALU.mult)
-            else:
-                nc.vector.tensor_tensor(out=v[:], in0=live["u", k][:], in1=c[:, :, 0:64], op=ALU.mult)
+            nc.vector.tensor_tensor(out=v[:], in0=live["u", k][:], in1=c[:], op=ALU.mult)
             live["v", k] = v
 
         def relu_sum(k):
@@ -163,14 +160,18 @@ def tile_dpfpattention_pa_kernel(tc, x, w_qk, out_0, out_1):
             unit, n, b, t = where(k)
             if t == 0 and half == 0:
                 live["o", unit] = o_pool.tile([P, 8, 4, P], F32, name="o")
-            nc.vector.scalar_tensor_tensor(
-                out=live["o", unit][:, :, t, 64 * half : 64 * (half + 1)],
-                in0=live["u", k][:],
-                scalar=0.0,
-                in1=live["wn", k][:],
-                op0=(ALU.is_gt if half == 0 else ALU.is_lt),
-                op1=ALU.mult,
-            )
+            o = live["o", unit]
+            if half == 1 and negative_on_gpsimd(k):
+                nc.gpsimd.tensor_tensor(out=o[:, :, t, 64:128], in0=live["wn", k][:], in1=o[:, :, t, 0:64], op=ALU.subtract)
+            else:
+                nc.vector.scalar_tensor_tensor(
+                    out=o[:, :, t, 64 * half : 64 * (half + 1)],
+                    in0=live["u", k][:],
+                    scalar=0.0,
+                    in1=live["wn", k][:],
+                    op0=(ALU.is_gt if half == 0 else ALU.is_lt),
+                    op1=ALU.mult,
+                )
 
         def store(k):
             unit, n, b, t = where(k)
@@ -219,8 +220,6 @@ def tile_dpfpattention_pa_kernel(tc, x, w_qk, out_0, out_1):
                     evacuate_x(0, t)
             if 2 <= s <= 5:
                 evacuate_x(1, s - 2)
-            if on(s) and cross_on_gpsimd(s):
-                cross(s)
             if on(s - 1):
                 relu_sum(s - 1)
             if on(s - 2):
@@ -228,7 +227,7 @@ def tile_dpfpattention_pa_kernel(tc, x, w_qk, out_0, out_1):
                 normalise(s - 2)
             if on(s - 4):
                 split(s - 4, 0)
-            if on(s) and not cross_on_gpsimd(s):
+            if on(s):
                 cross(s)
             if on(s - 4):
                 split(s - 4, 1)

@@ -23,7 +23,6 @@ def tile_dpfpattention_pa_kernel(tc, x, w_qk, out_0, out_1):
     outs = (out_0, out_1)
     with ExitStack() as ctx:
         keep = ctx.enter_context(tc.tile_pool(name="keep", bufs=1))
-        gx_pool = ctx.enter_context(tc.tile_pool(name="gx_pool", bufs=4))
         gw_pool = ctx.enter_context(tc.tile_pool(name="gw_pool", bufs=2))
         c_pool = ctx.enter_context(tc.tile_pool(name="c_pool", bufs=4))
         v_pool = ctx.enter_context(tc.tile_pool(name="v_pool", bufs=6))
@@ -38,10 +37,11 @@ def tile_dpfpattention_pa_kernel(tc, x, w_qk, out_0, out_1):
         warm = keep.tile([P, 8], F32, name="warm")
         x_sb = [keep.tile([P, 4, 1024], BF16, name="x_sb%d" % b) for b in range(2)]
         w_sb = [keep.tile([P, 2, 4, 512], BF16, name="w_sb%d" % n) for n in range(4)]
-        xq = [[keep.tile([P, 256], U32, name="xq%d%d" % (b, t), align_bytes=64) for t in range(4)] for b in range(2)]
-        xs = [[keep.tile([P, 256], U8, name="xs%d%d" % (b, t), align_bytes=64) for t in range(4)] for b in range(2)]
-        wq = [[keep.tile([P, 512], U32, name="wq%d%d" % (n, g), align_bytes=64) for g in range(2)] for n in range(4)]
-        ws = [[keep.tile([P, 512], U8, name="ws%d%d" % (n, g), align_bytes=64) for g in range(2)] for n in range(4)]
+        gx = [keep.tile([P, 4, 2, P, 4], BF16, name="gx%d" % b, align_bytes=64) for b in range(2)]
+        xq = [keep.tile([P, 4, 256], U32, name="xq%d" % b, align_bytes=64) for b in range(2)]
+        xs = [keep.tile([P, 4, 256], U8, name="xs%d" % b, align_bytes=64) for b in range(2)]
+        wq = [keep.tile([P, 2, 512], U32, name="wq%d" % n, align_bytes=64) for n in range(4)]
+        ws = [keep.tile([P, 2, 512], U8, name="ws%d" % n, align_bytes=64) for n in range(4)]
 
         live = {}
 
@@ -66,30 +66,28 @@ def tile_dpfpattention_pa_kernel(tc, x, w_qk, out_0, out_1):
             live["xt", b, t] = xt
 
         def evacuate_x(b, t):
-            gx = gx_pool.tile([P, 2, P, 4], BF16, name="gx", align_bytes=64)
-            nc.scalar.copy(out=gx[:].bitcast(F32), in_=live["xt", b, t][:].rearrange("p g u r -> p g r u"))
-            live["gx", b, t] = gx
+            nc.scalar.copy(out=gx[b][:, t].bitcast(F32), in_=live["xt", b, t][:].rearrange("p g u r -> p g r u"))
 
-        def quantise_x(b, t):
+        def quantise_x(b, t0, t1):
             nc.vector.quantize_mx(
-                out=xq[b][t][:].bitcast(FP8X4),
-                scales=xs[b][t][:],
-                in_=live["gx", b, t][:].rearrange("p g r j -> p (g r j)"),
+                out=xq[b][:, t0:t1, :].rearrange("p t c -> p (t c)").bitcast(FP8X4),
+                scales=xs[b][:, t0:t1, :].rearrange("p t c -> p (t c)"),
+                in_=gx[b][:, t0:t1].rearrange("p t g r j -> p (t g r j)"),
             )
 
-        def regroup_w(n, g):
-            if g == 0:
+        def regroup_w(n, g0, g1):
+            if g0 == 0:
                 live["gw", n] = gw_pool.tile([P, 2, 512, 4], BF16, name="gw", align_bytes=64)
             nc.vector.tensor_copy(
-                out=live["gw", n][:, g].rearrange("p (c i) j -> p c j i", i=4),
-                in_=w_sb[n][:, g].rearrange("p j (c i) -> p c j i", i=4),
+                out=live["gw", n][:, g0:g1].rearrange("p g (c i) j -> p g c j i", i=4),
+                in_=w_sb[n][:, g0:g1].rearrange("p g j (c i) -> p g c j i", i=4),
             )
 
-        def quantise_w(n, g):
+        def quantise_w(n, g0, g1):
             nc.vector.quantize_mx(
-                out=wq[n][g][:].bitcast(FP8X4),
-                scales=ws[n][g][:],
-                in_=live["gw", n][:, g].rearrange("p c j -> p (c j)"),
+                out=wq[n][:, g0:g1, :].rearrange("p g c -> p (g c)").bitcast(FP8X4),
+                scales=ws[n][:, g0:g1, :].rearrange("p g c -> p (g c)"),
+                in_=live["gw", n][:, g0:g1].rearrange("p g c j -> p (g c j)"),
             )
 
         def negative_on_gpsimd(k):
@@ -109,10 +107,10 @@ def tile_dpfpattention_pa_kernel(tc, x, w_qk, out_0, out_1):
             for g in range(2):
                 nc.tensor.matmul_mx(
                     out=u[:].rearrange("p h d -> p (h d)"),
-                    lhsT=xq[b][t][:, P * g : P * (g + 1)].bitcast(FP8X4),
-                    lhsT_scale=xs[b][t][:, P * g : P * (g + 1)],
-                    rhs=wq[n][g][:].bitcast(FP8X4),
-                    rhs_scale=ws[n][g][:],
+                    lhsT=xq[b][:, t, P * g : P * (g + 1)].bitcast(FP8X4),
+                    lhsT_scale=xs[b][:, t, P * g : P * (g + 1)],
+                    rhs=wq[n][:, g, :].bitcast(FP8X4),
+                    rhs_scale=ws[n][:, g, :],
                     start=(g == 0),
                     stop=(g == 1),
                 )
@@ -200,11 +198,11 @@ def tile_dpfpattention_pa_kernel(tc, x, w_qk, out_0, out_1):
 
         transpose_x(0, 0)
         evacuate_x(0, 0)
-        regroup_w(0, 0)
-        quantise_x(0, 0)
-        regroup_w(0, 1)
-        quantise_w(0, 0)
-        quantise_w(0, 1)
+        regroup_w(0, 0, 1)
+        quantise_x(0, 0, 1)
+        regroup_w(0, 1, 2)
+        quantise_w(0, 0, 1)
+        quantise_w(0, 1, 2)
         multiply(0)
         for t in range(1, 4):
             transpose_x(0, t)
@@ -218,8 +216,9 @@ def tile_dpfpattention_pa_kernel(tc, x, w_qk, out_0, out_1):
             if s == 0:
                 for t in range(1, 4):
                     evacuate_x(0, t)
-            if 2 <= s <= 5:
-                evacuate_x(1, s - 2)
+            if 1 <= s <= 2:
+                evacuate_x(1, 2 * s - 2)
+                evacuate_x(1, 2 * s - 1)
             if on(s - 1):
                 relu_sum(s - 1)
             if on(s - 2):
@@ -233,19 +232,17 @@ def tile_dpfpattention_pa_kernel(tc, x, w_qk, out_0, out_1):
                 split(s - 4, 1)
                 store(s - 4)
             if s == 0:
-                for t in range(1, 4):
-                    quantise_x(0, t)
+                quantise_x(0, 1, 2)
+                quantise_x(0, 2, 4)
                 multiply(1)
-            if 2 <= s <= 5:
-                quantise_x(1, s - 2)
-            n, piece = divmod(s + 6, 8)
-            if 1 <= n <= 3 and piece < 4:
-                if piece < 2:
-                    regroup_w(n, piece)
-                else:
-                    quantise_w(n, piece - 2)
+            if s == 2:
+                quantise_x(1, 0, 4)
+            n, piece = divmod(s + 5, 8)
+            if 1 <= n <= 3 and piece == 0:
+                regroup_w(n, 0, 2)
+                quantise_w(n, 0, 2)
             if on(s + 2):
                 multiply(s + 2)
-            if s == 1:
+            if s == 0:
                 for t in range(4):
                     transpose_x(1, t)

@@ -183,12 +183,14 @@ def tile_dpfpattention_pa_kernel(tc, x, w_qk, out_0, out_1):
                     in_=o[:].rearrange("p h t f -> p h (t f)"),
                 )
 
-        load_x(0, 0, 1)
         load_w(0, 0)
+        load_x(0, 0, 1)
         load_w(0, 1)
         load_x(0, 1, 4)
+        load_w(1, 0)
+        load_w(1, 1)
         load_x(1, 0, 4)
-        for n in range(1, 4):
+        for n in range(2, 4):
             load_w(n, 0)
             load_w(n, 1)
 
@@ -199,13 +201,15 @@ def tile_dpfpattention_pa_kernel(tc, x, w_qk, out_0, out_1):
         transpose_x(0, 0)
         evacuate_x(0, 0)
         regroup_w(0, 0, 1)
-        quantise_x(0, 0, 1)
-        regroup_w(0, 1, 2)
         quantise_w(0, 0, 1)
+        regroup_w(0, 1, 2)
+        quantise_x(0, 0, 1)
         quantise_w(0, 1, 2)
+        transpose_x(0, 1)
         multiply(0)
-        for t in range(1, 4):
-            transpose_x(0, t)
+        transpose_x(0, 2)
+        transpose_x(0, 3)
+        evacuate_x(0, 1)
 
         def on(k):
             return 0 <= k < N_BANKS
@@ -214,8 +218,8 @@ def tile_dpfpattention_pa_kernel(tc, x, w_qk, out_0, out_1):
             if on(s):
                 roll(s)
             if s == 0:
-                for t in range(1, 4):
-                    evacuate_x(0, t)
+                evacuate_x(0, 2)
+                evacuate_x(0, 3)
             if 1 <= s <= 2:
                 evacuate_x(1, 2 * s - 2)
                 evacuate_x(1, 2 * s - 1)
@@ -233,14 +237,19 @@ def tile_dpfpattention_pa_kernel(tc, x, w_qk, out_0, out_1):
                 store(s - 4)
             if s == 0:
                 quantise_x(0, 1, 2)
-                quantise_x(0, 2, 4)
                 multiply(1)
+                quantise_x(0, 2, 4)
+                regroup_w(1, 0, 2)
+            if s == 1:
+                quantise_w(1, 0, 2)
             if s == 2:
                 quantise_x(1, 0, 4)
-            n, piece = divmod(s + 5, 8)
-            if 1 <= n <= 3 and piece == 0:
-                regroup_w(n, 0, 2)
-                quantise_w(n, 0, 2)
+                regroup_w(2, 0, 2)
+            if s == 3:
+                quantise_w(2, 0, 2)
+            if s == 4:
+                regroup_w(3, 0, 2)
+                quantise_w(3, 0, 2)
             if on(s + 2):
                 multiply(s + 2)
             if s == 0:

@@ -177,10 +177,10 @@ def tile_dpfpattention_pa_kernel(tc, x, w_qk, out_0, out_1):
             o = live["o", unit]
             if unit == 7:
                 nc.sync.dma_start(out=heads.rearrange("h (p t) f -> t p h f", t=4)[t], in_=o[:, :, t, :])
-            elif t == 3:
+            elif t % 2 == 1:
                 nc.sync.dma_start(
-                    out=heads.rearrange("h (p t) f -> p h (t f)", t=4),
-                    in_=o[:].rearrange("p h t f -> p h (t f)"),
+                    out=heads.rearrange("h (p t) f -> p h t f", t=4)[:, :, t - 1 : t + 1, :],
+                    in_=o[:, :, t - 1 : t + 1, :],
                 )
 
         load_w(0, 0)

@@ -75,10 +75,10 @@ def tile_dpfpattention_pa_kernel(tc, x, w_qk, out_0, out_1):
                 in_=gx[b][:, t0:t1].rearrange("p t g r j -> p (t g r j)"),
             )
 
-        def regroup_w(n, g0, g1):
+        def regroup_w(n, g0, g1, copy=nc.vector.tensor_copy):
             if g0 == 0:
                 live["gw", n] = gw_pool.tile([P, 2, 512, 4], BF16, name="gw", align_bytes=64)
-            nc.vector.tensor_copy(
+            copy(
                 out=live["gw", n][:, g0:g1].rearrange("p g (c i) j -> p g c j i", i=4),
                 in_=w_sb[n][:, g0:g1].rearrange("p g j (c i) -> p g c j i", i=4),
             )
@@ -91,10 +91,10 @@ def tile_dpfpattention_pa_kernel(tc, x, w_qk, out_0, out_1):
             )
 
         def negative_on_gpsimd(k):
-            return k % 2 == 0
+            return k % 5 == 1 and k < 28
 
         def normalise_on_scalar(k):
-            return k % 4 == 0
+            return False
 
         def where(k):
             unit, t = divmod(k, 4)
@@ -223,6 +223,10 @@ def tile_dpfpattention_pa_kernel(tc, x, w_qk, out_0, out_1):
             if 1 <= s <= 2:
                 evacuate_x(1, 2 * s - 2)
                 evacuate_x(1, 2 * s - 1)
+            if s == 3:
+                regroup_w(2, 1, 2, nc.scalar.copy)
+            if s == 5:
+                regroup_w(3, 1, 2, nc.scalar.copy)
             if on(s - 1):
                 relu_sum(s - 1)
             if on(s - 2):
@@ -244,11 +248,12 @@ def tile_dpfpattention_pa_kernel(tc, x, w_qk, out_0, out_1):
                 quantise_w(1, 0, 2)
             if s == 2:
                 quantise_x(1, 0, 4)
-                regroup_w(2, 0, 2)
+                regroup_w(2, 0, 1)
             if s == 3:
                 quantise_w(2, 0, 2)
             if s == 4:
-                regroup_w(3, 0, 2)
+                regroup_w(3, 0, 1)
+            if s == 5:
                 quantise_w(3, 0, 2)
             if on(s + 2):
                 multiply(s + 2)

@@ -25,7 +25,8 @@ def tile_dpfpattention_pa_kernel(tc, x, w_qk, out_0, out_1):
         keep = ctx.enter_context(tc.tile_pool(name="keep", bufs=1))
         gw_pool = ctx.enter_context(tc.tile_pool(name="gw_pool", bufs=2))
         c_pool = ctx.enter_context(tc.tile_pool(name="c_pool", bufs=4))
-        v_pool = ctx.enter_context(tc.tile_pool(name="v_pool", bufs=6))
+        x_pool = ctx.enter_context(tc.tile_pool(name="x_pool", bufs=3))
+        v_pool = ctx.enter_context(tc.tile_pool(name="v_pool", bufs=5))
         wn_pool = ctx.enter_context(tc.tile_pool(name="wn_pool", bufs=5))
         stat_pool = ctx.enter_context(tc.tile_pool(name="stat_pool", bufs=6))
         o_pool = ctx.enter_context(tc.tile_pool(name="o_pool", bufs=3))
@@ -91,10 +92,10 @@ def tile_dpfpattention_pa_kernel(tc, x, w_qk, out_0, out_1):
             )
 
         def negative_on_gpsimd(k):
-            return k % 5 == 1 and k < 28
+            return k % 2 == 0 and k < 28
 
         def normalise_on_scalar(k):
-            return False
+            return k % 3 == 0
 
         def where(k):
             unit, t = divmod(k, 4)
@@ -118,22 +119,31 @@ def tile_dpfpattention_pa_kernel(tc, x, w_qk, out_0, out_1):
 
         def roll(k):
             u = live["u", k]
-            c = c_pool.tile([P, 8, 64], F32, name="c")
-            nc.scalar.copy(out=c[:, :, 1:64], in_=u[:, :, 0:63])
+            c = c_pool.tile([P, 8, 33], F32, name="c")
+            nc.scalar.copy(out=c[:, :, 1:33], in_=u[:, :, 1:64:2])
             nc.scalar.mul(out=c[:, :, 0:1], in_=u[:, :, 63:64], mul=-1.0)
             live["c", k] = c
 
         def cross(k):
-            v = v_pool.tile([P, 8, 64], F32, name="v")
+            x2 = x_pool.tile([P, 8, 2, 32], F32, name="x2")
             c = live["c", k]
-            nc.vector.tensor_tensor(out=v[:], in0=live["u", k][:], in1=c[:], op=ALU.mult)
-            live["v", k] = v
+            even = live["u", k][:, :, 0:64:2]
+            nc.vector.tensor_tensor(out=x2[:, :, 0, :], in0=even, in1=c[:, :, 0:32], op=ALU.mult)
+            nc.vector.tensor_tensor(out=x2[:, :, 1, :], in0=even, in1=c[:, :, 1:33], op=ALU.mult)
+            live["x2", k] = x2
 
         def relu_sum(k):
-            v = live["v", k]
+            x2 = live["x2", k]
+            v = v_pool.tile([P, 8, 64], F32, name="v")
             ssum = stat_pool.tile([P, 8], F32, name="ssum")
             for h in range(8):
-                nc.scalar.activation(out=v[:, h, :], in_=v[:, h, :], func=ACT.Relu, accum_out=ssum[:, h : h + 1])
+                nc.scalar.activation(
+                    out=v[:, h, :].rearrange("p (i a) -> p i a", a=2),
+                    in_=x2[:, h].rearrange("p a i -> p i a"),
+                    func=ACT.Relu,
+                    accum_out=ssum[:, h : h + 1],
+                )
+            live["v", k] = v
             live["ssum", k] = ssum
 
         def invert(k):
@@ -175,7 +185,7 @@ def tile_dpfpattention_pa_kernel(tc, x, w_qk, out_0, out_1):
             unit, n, b, t = where(k)
             heads = outs[n // 2][b, 8 * (n % 2) : 8 * (n % 2) + 8]
             o = live["o", unit]
-            if unit == 7:
+            if k >= N_BANKS - 2:
                 nc.sync.dma_start(out=heads.rearrange("h (p t) f -> t p h f", t=4)[t], in_=o[:, :, t, :])
             elif t % 2 == 1:
                 nc.sync.dma_start(
@@ -220,10 +230,10 @@ def tile_dpfpattention_pa_kernel(tc, x, w_qk, out_0, out_1):
             if s == 0:
                 evacuate_x(0, 2)
                 evacuate_x(0, 3)
-            if 1 <= s <= 2:
-                evacuate_x(1, 2 * s - 2)
-                evacuate_x(1, 2 * s - 1)
-            if s == 3:
+            if s == 2:
+                for t in range(4):
+                    evacuate_x(1, t)
+            if s == 4:
                 regroup_w(2, 1, 2, nc.scalar.copy)
             if s == 5:
                 regroup_w(3, 1, 2, nc.scalar.copy)
@@ -249,10 +259,9 @@ def tile_dpfpattention_pa_kernel(tc, x, w_qk, out_0, out_1):
             if s == 2:
                 quantise_x(1, 0, 4)
                 regroup_w(2, 0, 1)
-            if s == 3:
-                quantise_w(2, 0, 2)
-            if s == 4:
                 regroup_w(3, 0, 1)
+            if s == 4:
+                quantise_w(2, 0, 2)
             if s == 5:
                 quantise_w(3, 0, 2)
             if on(s + 2):

@@ -119,17 +119,17 @@ def tile_dpfpattention_pa_kernel(tc, x, w_qk, out_0, out_1):
 
         def roll(k):
             u = live["u", k]
-            c = c_pool.tile([P, 8, 33], F32, name="c")
-            nc.scalar.copy(out=c[:, :, 1:33], in_=u[:, :, 1:64:2])
-            nc.scalar.mul(out=c[:, :, 0:1], in_=u[:, :, 63:64], mul=-1.0)
+            c = c_pool.tile([P, 8, 36], F32, name="c")
+            nc.scalar.copy(out=c[:, :, 4:36], in_=u[:, :, 1:64:2])
+            nc.scalar.mul(out=c[:, :, 0:4], in_=u[:, :, 60:64], mul=-1.0)
             live["c", k] = c
 
         def cross(k):
             x2 = x_pool.tile([P, 8, 2, 32], F32, name="x2")
             c = live["c", k]
             even = live["u", k][:, :, 0:64:2]
-            nc.vector.tensor_tensor(out=x2[:, :, 0, :], in0=even, in1=c[:, :, 0:32], op=ALU.mult)
-            nc.vector.tensor_tensor(out=x2[:, :, 1, :], in0=even, in1=c[:, :, 1:33], op=ALU.mult)
+            nc.vector.tensor_tensor(out=x2[:, :, 0, :], in0=even, in1=c[:, :, 3:35], op=ALU.mult)
+            nc.vector.tensor_tensor(out=x2[:, :, 1, :], in0=even, in1=c[:, :, 4:36], op=ALU.mult)
             live["x2", k] = x2
 
         def relu_sum(k):

@@ -185,7 +185,7 @@ def tile_dpfpattention_pa_kernel(tc, x, w_qk, out_0, out_1):
             unit, n, b, t = where(k)
             heads = outs[n // 2][b, 8 * (n % 2) : 8 * (n % 2) + 8]
             o = live["o", unit]
-            if k >= N_BANKS - 2:
+            if k >= N_BANKS - 6:
                 nc.sync.dma_start(out=heads.rearrange("h (p t) f -> t p h f", t=4)[t], in_=o[:, :, t, :])
             elif t % 2 == 1:
                 nc.sync.dma_start(

@@ -35,6 +35,7 @@ def tile_dpfpattention_pa_kernel(tc, x, w_qk, out_0, out_1):
             ctx.enter_context(tc.manual_schedule())
 
         ident = keep.tile([P, P], F32, name="ident")
+        ident16 = keep.tile([P, P], BF16, name="ident16")
         warm = keep.tile([P, 8], F32, name="warm")
         x_sb = [keep.tile([P, 4, 1024], BF16, name="x_sb%d" % b) for b in range(2)]
         w_sb = [keep.tile([P, 2, 4, 512], BF16, name="w_sb%d" % n) for n in range(4)]
@@ -82,6 +83,27 @@ def tile_dpfpattention_pa_kernel(tc, x, w_qk, out_0, out_1):
             copy(
                 out=live["gw", n][:, g0:g1].rearrange("p g (c i) j -> p g c j i", i=4),
                 in_=w_sb[n][:, g0:g1].rearrange("p g j (c i) -> p g c j i", i=4),
+            )
+
+        def interleave_w(n, g, half):
+            wt = psum.tile([P, 2, 128, 4], BF16, name="wt", tag="bank")
+            for i in range(2):
+                c0 = 256 * half + 128 * i
+                nc.tensor.matmul(
+                    out=wt[:, i].rearrange("p c j -> p (c j)"),
+                    lhsT=ident16[:],
+                    rhs=w_sb[n][:, g, :, c0 : c0 + 128].rearrange("p j c -> p c j"),
+                    start=True,
+                    stop=True,
+                )
+            live["wt", n, g, half] = wt
+
+        def evacuate_w(n, g, half):
+            if ("gw", n) not in live:
+                live["gw", n] = gw_pool.tile([P, 2, 512, 4], BF16, name="gw", align_bytes=64)
+            nc.scalar.copy(
+                out=live["gw", n][:, g, 256 * half : 256 * (half + 1), :],
+                in_=live["wt", n, g, half][:].rearrange("p i c j -> p (i c) j"),
             )
 
         def quantise_w(n, g0, g1):
@@ -198,13 +220,15 @@ def tile_dpfpattention_pa_kernel(tc, x, w_qk, out_0, out_1):
         load_w(0, 1)
         load_x(0, 1, 4)
         load_w(1, 0)
+        load_x(1, 0, 2)
         load_w(1, 1)
-        load_x(1, 0, 4)
+        load_x(1, 2, 4)
         for n in range(2, 4):
             load_w(n, 0)
             load_w(n, 1)
 
         masks.make_identity(nc, ident[:])
+        masks.make_identity(nc, ident16[:])
         nc.vector.memset(warm[:], 0.0)
         nc.scalar.activation(out=warm[:], in_=warm[:], func=ACT.Relu)
 
@@ -224,6 +248,9 @@ def tile_dpfpattention_pa_kernel(tc, x, w_qk, out_0, out_1):
         def on(k):
             return 0 <= k < N_BANKS
 
+        def quarter(i):
+            return 2 + i // 4, (i // 2) % 2, i % 2
+
         for s in range(N_BANKS + 5):
             if on(s):
                 roll(s)
@@ -233,10 +260,8 @@ def tile_dpfpattention_pa_kernel(tc, x, w_qk, out_0, out_1):
             if s == 2:
                 for t in range(4):
                     evacuate_x(1, t)
-            if s == 4:
-                regroup_w(2, 1, 2, nc.scalar.copy)
-            if s == 5:
-                regroup_w(3, 1, 2, nc.scalar.copy)
+            if 8 <= s < 16:
+                evacuate_w(*quarter(s - 8))
             if on(s - 1):
                 relu_sum(s - 1)
             if on(s - 2):
@@ -258,14 +283,13 @@ def tile_dpfpattention_pa_kernel(tc, x, w_qk, out_0, out_1):
                 quantise_w(1, 0, 2)
             if s == 2:
                 quantise_x(1, 0, 4)
-                regroup_w(2, 0, 1)
-                regroup_w(3, 0, 1)
-            if s == 4:
-                quantise_w(2, 0, 2)
-            if s == 5:
-                quantise_w(3, 0, 2)
+            if 8 <= s < 16 and s % 2 == 1:
+                n, g, half = quarter(s - 8)
+                quantise_w(n, g, g + 1)
             if on(s + 2):
                 multiply(s + 2)
+            if 6 <= s < 14:
+                interleave_w(*quarter(s - 6))
             if s == 0:
                 for t in range(4):
                     transpose_x(1, t)

@@ -98,10 +98,10 @@ def tile_dpfpattention_pa_kernel(tc, x, w_qk, out_0, out_1):
                 )
             live["wt", n, g, half] = wt
 
-        def evacuate_w(n, g, half):
+        def evacuate_w(n, g, half, copy):
             if ("gw", n) not in live:
                 live["gw", n] = gw_pool.tile([P, 2, 512, 4], BF16, name="gw", align_bytes=64)
-            nc.scalar.copy(
+            copy(
                 out=live["gw", n][:, g, 256 * half : 256 * (half + 1), :],
                 in_=live["wt", n, g, half][:].rearrange("p i c j -> p (i c) j"),
             )
@@ -117,7 +117,7 @@ def tile_dpfpattention_pa_kernel(tc, x, w_qk, out_0, out_1):
             return k % 2 == 0 and k < 28
 
         def normalise_on_scalar(k):
-            return k % 3 == 0
+            return k % (2 if 8 <= k < 16 else 3) == 0
 
         def where(k):
             unit, t = divmod(k, 4)
@@ -260,8 +260,8 @@ def tile_dpfpattention_pa_kernel(tc, x, w_qk, out_0, out_1):
             if s == 2:
                 for t in range(4):
                     evacuate_x(1, t)
-            if 8 <= s < 16:
-                evacuate_w(*quarter(s - 8))
+            if 8 <= s < 16 and s % 2 == 1:
+                evacuate_w(*quarter(s - 8), nc.scalar.copy)
             if on(s - 1):
                 relu_sum(s - 1)
             if on(s - 2):
@@ -283,6 +283,8 @@ def tile_dpfpattention_pa_kernel(tc, x, w_qk, out_0, out_1):
                 quantise_w(1, 0, 2)
             if s == 2:
                 quantise_x(1, 0, 4)
+            if 8 <= s < 16 and s % 2 == 0:
+                evacuate_w(*quarter(s - 8), nc.vector.tensor_copy)
             if 8 <= s < 16 and s % 2 == 1:
                 n, g, half = quarter(s - 8)
                 quantise_w(n, g, g + 1)

from contextlib import ExitStack

import concourse.masks as masks
import concourse.mybir as mybir

FLOPS = 2 * 1024 * 1024 * 2048

F32 = mybir.dt.float32
BF16 = mybir.dt.bfloat16
U32 = mybir.dt.uint32
U8 = mybir.dt.uint8
FP8X4 = mybir.dt.float8_e4m3fn_x4
ALU = mybir.AluOpType
ACT = mybir.ActivationFunctionType

P = 128
PINNED = True
N_BANKS = 32


def tile_dpfpattention_pa_kernel(tc, x, w_qk, out_0, out_1):
    nc = tc.nc
    outs = (out_0, out_1)
    with ExitStack() as ctx:
        keep = ctx.enter_context(tc.tile_pool(name="keep", bufs=1))
        gw_pool = ctx.enter_context(tc.tile_pool(name="gw_pool", bufs=2))
        c_pool = ctx.enter_context(tc.tile_pool(name="c_pool", bufs=4))
        x_pool = ctx.enter_context(tc.tile_pool(name="x_pool", bufs=3))
        v_pool = ctx.enter_context(tc.tile_pool(name="v_pool", bufs=5))
        wn_pool = ctx.enter_context(tc.tile_pool(name="wn_pool", bufs=5))
        stat_pool = ctx.enter_context(tc.tile_pool(name="stat_pool", bufs=6))
        o_pool = ctx.enter_context(tc.tile_pool(name="o_pool", bufs=3))
        psum = ctx.enter_context(tc.psum_pool(name="psum", bufs=8))
        if PINNED:
            ctx.enter_context(tc.manual_schedule())

        ident = keep.tile([P, P], F32, name="ident")
        ident16 = keep.tile([P, P], BF16, name="ident16")
        warm = keep.tile([P, 8], F32, name="warm")
        x_sb = [keep.tile([P, 4, 1024], BF16, name="x_sb%d" % b) for b in range(2)]
        w_sb = [keep.tile([P, 2, 4, 512], BF16, name="w_sb%d" % n) for n in range(4)]
        gx = [keep.tile([P, 4, 2, P, 4], BF16, name="gx%d" % b, align_bytes=64) for b in range(2)]
        xq = [keep.tile([P, 4, 256], U32, name="xq%d" % b, align_bytes=64) for b in range(2)]
        xs = [keep.tile([P, 4, 256], U8, name="xs%d" % b, align_bytes=64) for b in range(2)]
        wq = [keep.tile([P, 2, 512], U32, name="wq%d" % n, align_bytes=64) for n in range(4)]
        ws = [keep.tile([P, 2, 512], U8, name="ws%d" % n, align_bytes=64) for n in range(4)]

        live = {}

        def load_x(b, t0, t1):
            nc.sync.dma_start(
                out=x_sb[b][:, t0:t1, :],
                in_=x[b].rearrange("(p t) k -> p t k", t=4)[:, t0:t1, :],
            )

        def load_w(n, g):
            nc.sync.dma_start(
                out=w_sb[n][:, g],
                in_=w_qk[512 * g : 512 * (g + 1), 512 * n : 512 * (n + 1)].rearrange("(p j) c -> p j c", j=4),
            )

        def transpose_x(b, t):
            xt = psum.tile([P, 2, 2, P], F32, name="xt", tag="bank")
            words = x_sb[b][:, t, :].bitcast(F32)
            for g in range(2):
                for u in range(2):
                    nc.tensor.transpose(xt[:, g, u, :], words[:, 256 * g + u : 256 * (g + 1) : 2], ident[:])
            live["xt", b, t] = xt

        def evacuate_x(b, t):
            nc.scalar.copy(out=gx[b][:, t].bitcast(F32), in_=live["xt", b, t][:].rearrange("p g u r -> p g r u"))

        def quantise_x(b, t0, t1):
            nc.vector.quantize_mx(
                out=xq[b][:, t0:t1, :].rearrange("p t c -> p (t c)").bitcast(FP8X4),
                scales=xs[b][:, t0:t1, :].rearrange("p t c -> p (t c)"),
                in_=gx[b][:, t0:t1].rearrange("p t g r j -> p (t g r j)"),
            )

        def regroup_w(n, g0, g1, copy=nc.vector.tensor_copy):
            if g0 == 0:
                live["gw", n] = gw_pool.tile([P, 2, 512, 4], BF16, name="gw", align_bytes=64)
            copy(
                out=live["gw", n][:, g0:g1].rearrange("p g (c i) j -> p g c j i", i=4),
                in_=w_sb[n][:, g0:g1].rearrange("p g j (c i) -> p g c j i", i=4),
            )

        def interleave_w(n, g, half):
            wt = psum.tile([P, 2, 128, 4], BF16, name="wt", tag="bank")
            for i in range(2):
                c0 = 256 * half + 128 * i
                nc.tensor.matmul(
                    out=wt[:, i].rearrange("p c j -> p (c j)"),
                    lhsT=ident16[:],
                    rhs=w_sb[n][:, g, :, c0 : c0 + 128].rearrange("p j c -> p c j"),
                    start=True,
                    stop=True,
                )
            live["wt", n, g, half] = wt

        def evacuate_w(n, g, half, copy):
            if ("gw", n) not in live:
                live["gw", n] = gw_pool.tile([P, 2, 512, 4], BF16, name="gw", align_bytes=64)
            copy(
                out=live["gw", n][:, g, 256 * half : 256 * (half + 1), :],
                in_=live["wt", n, g, half][:].rearrange("p i c j -> p (i c) j"),
            )

        def quantise_w(n, g0, g1):
            nc.vector.quantize_mx(
                out=wq[n][:, g0:g1, :].rearrange("p g c -> p (g c)").bitcast(FP8X4),
                scales=ws[n][:, g0:g1, :].rearrange("p g c -> p (g c)"),
                in_=live["gw", n][:, g0:g1].rearrange("p g c j -> p (g c j)"),
            )

        def negative_on_gpsimd(k):
            return k % 2 == 0 and k < 28

        def normalise_on_scalar(k):
            return k % (2 if 8 <= k < 16 else 3) == 0

        def where(k):
            unit, t = divmod(k, 4)
            n, b = divmod(unit, 2)
            return unit, n, b, t

        def multiply(k):
            unit, n, b, t = where(k)
            u = psum.tile([P, 8, 64], F32, name="u", tag="bank")
            for g in range(2):
                nc.tensor.matmul_mx(
                    out=u[:].rearrange("p h d -> p (h d)"),
                    lhsT=xq[b][:, t, P * g : P * (g + 1)].bitcast(FP8X4),
                    lhsT_scale=xs[b][:, t, P * g : P * (g + 1)],
                    rhs=wq[n][:, g, :].bitcast(FP8X4),
                    rhs_scale=ws[n][:, g, :],
                    start=(g == 0),
                    stop=(g == 1),
                )
            live["u", k] = u

        def roll(k):
            u = live["u", k]
            c = c_pool.tile([P, 8, 36], F32, name="c")
            nc.scalar.copy(out=c[:, :, 4:36], in_=u[:, :, 1:64:2])
            nc.scalar.mul(out=c[:, :, 0:4], in_=u[:, :, 60:64], mul=-1.0)
            live["c", k] = c

        def cross(k):
            x2 = x_pool.tile([P, 8, 2, 32], F32, name="x2")
            c = live["c", k]
            even = live["u", k][:, :, 0:64:2]
            nc.vector.tensor_tensor(out=x2[:, :, 0, :], in0=even, in1=c[:, :, 3:35], op=ALU.mult)
            nc.vector.tensor_tensor(out=x2[:, :, 1, :], in0=even, in1=c[:, :, 4:36], op=ALU.mult)
            live["x2", k] = x2

        def relu_sum(k):
            x2 = live["x2", k]
            v = v_pool.tile([P, 8, 64], F32, name="v")
            ssum = stat_pool.tile([P, 8], F32, name="ssum")
            for h in range(8):
                nc.scalar.activation(
                    out=v[:, h, :].rearrange("p (i a) -> p i a", a=2),
                    in_=x2[:, h].rearrange("p a i -> p i a"),
                    func=ACT.Relu,
                    accum_out=ssum[:, h : h + 1],
                )
            live["v", k] = v
            live["ssum", k] = ssum

        def invert(k):
            rinv = stat_pool.tile([P, 8], F32, name="rinv")
            nc.vector.reciprocal(out=rinv[:], in_=live["ssum", k][:])
            live["rinv", k] = rinv

        def normalise(k):
            wn = wn_pool.tile([P, 8, 64], F32, name="wn")
            v = live["v", k]
            rinv = live["rinv", k]
            if normalise_on_scalar(k):
                for h in range(8):
                    nc.scalar.activation(out=wn[:, h, :], in_=v[:, h, :], func=ACT.Copy, scale=rinv[:, h : h + 1])
            else:
                nc.gpsimd.tensor_tensor(
                    out=wn[:], in0=v[:], in1=rinv[:].unsqueeze(2).to_broadcast([P, 8, 64]), op=ALU.mult
                )
            live["wn", k] = wn

        def split(k, half):
            unit, n, b, t = where(k)
            if t == 0 and half == 0:
                live["o", unit] = o_pool.tile([P, 8, 4, P], F32, name="o")
            o = live["o", unit]
            if half == 1 and negative_on_gpsimd(k):
                nc.gpsimd.tensor_tensor(out=o[:, :, t, 64:128], in0=live["wn", k][:], in1=o[:, :, t, 0:64], op=ALU.subtract)
            else:
                nc.vector.scalar_tensor_tensor(
                    out=o[:, :, t, 64 * half : 64 * (half + 1)],
                    in0=live["u", k][:],
                    scalar=0.0,
                    in1=live["wn", k][:],
                    op0=(ALU.is_gt if half == 0 else ALU.is_lt),
                    op1=ALU.mult,
                )

        def store(k):
            unit, n, b, t = where(k)
            heads = outs[n // 2][b, 8 * (n % 2) : 8 * (n % 2) + 8]
            o = live["o", unit]
            if k >= N_BANKS - 6:
                nc.sync.dma_start(out=heads.rearrange("h (p t) f -> t p h f", t=4)[t], in_=o[:, :, t, :])
            elif t % 2 == 1:
                nc.sync.dma_start(
                    out=heads.rearrange("h (p t) f -> p h t f", t=4)[:, :, t - 1 : t + 1, :],
                    in_=o[:, :, t - 1 : t + 1, :],
                )

        load_w(0, 0)
        load_x(0, 0, 1)
        load_w(0, 1)
        load_x(0, 1, 4)
        load_w(1, 0)
        load_x(1, 0, 2)
        load_w(1, 1)
        load_x(1, 2, 4)
        for n in range(2, 4):
            load_w(n, 0)
            load_w(n, 1)

        masks.make_identity(nc, ident[:])
        masks.make_identity(nc, ident16[:])
        nc.vector.memset(warm[:], 0.0)
        nc.scalar.activation(out=warm[:], in_=warm[:], func=ACT.Relu)

        transpose_x(0, 0)
        evacuate_x(0, 0)
        regroup_w(0, 0, 1)
        quantise_w(0, 0, 1)
        regroup_w(0, 1, 2)
        quantise_x(0, 0, 1)
        quantise_w(0, 1, 2)
        transpose_x(0, 1)
        multiply(0)
        transpose_x(0, 2)
        transpose_x(0, 3)
        evacuate_x(0, 1)

        def on(k):
            return 0 <= k < N_BANKS

        def quarter(i):
            return 2 + i // 4, (i // 2) % 2, i % 2

        for s in range(N_BANKS + 5):
            if on(s):
                roll(s)
            if s == 0:
                evacuate_x(0, 2)
                evacuate_x(0, 3)
            if s == 2:
                for t in range(4):
                    evacuate_x(1, t)
            if 8 <= s < 16 and s % 2 == 1:
                evacuate_w(*quarter(s - 8), nc.scalar.copy)
            if on(s - 1):
                relu_sum(s - 1)
            if on(s - 2):
                invert(s - 2)
                normalise(s - 2)
            if on(s - 4):
                split(s - 4, 0)
            if on(s):
                cross(s)
            if on(s - 4):
                split(s - 4, 1)
                store(s - 4)
            if s == 0:
                quantise_x(0, 1, 2)
                multiply(1)
                quantise_x(0, 2, 4)
                regroup_w(1, 0, 2)
            if s == 1:
                quantise_w(1, 0, 2)
            if s == 2:
                quantise_x(1, 0, 4)
            if 8 <= s < 16 and s % 2 == 0:
                evacuate_w(*quarter(s - 8), nc.vector.tensor_copy)
            if 8 <= s < 16 and s % 2 == 1:
                n, g, half = quarter(s - 8)
                quantise_w(n, g, g + 1)
            if on(s + 2):
                multiply(s + 2)
            if 6 <= s < 14:
                interleave_w(*quarter(s - 6))
            if s == 0:
                for t in range(4):
                    transpose_x(1, t)
